import numpy as np
import ml_dtypes


def mxq(x, axis, fmt="e4m3"):
    dtype, down = {"e4m3": (ml_dtypes.float8_e4m3fn, 7), "e5m2": (ml_dtypes.float8_e5m2, 14)}[fmt]
    v = np.moveaxis(np.asarray(x, np.float32).astype(ml_dtypes.bfloat16).astype(np.float64), axis, -1)
    blocks = v.reshape(v.shape[:-1] + (-1, 32))
    amax = np.abs(blocks).max(-1, keepdims=True)
    byte = np.maximum(np.where(amax > 0, np.frexp(amax)[1] - 1 + 127, 0) - down, 1)
    scale = np.exp2(byte - 127.0)
    codes = (blocks / scale).astype(np.float32).astype(dtype).astype(np.float64)
    return np.moveaxis((codes * scale).reshape(v.shape), -1, axis)


WIDE = False


def mx_kscale(k):
    if not WIDE:
        return np.ones(k)
    levels = np.array([10, -10, 5, -5, 0])
    if k % 512:
        return np.exp2(np.random.permutation(np.resize(levels, k // 32))).repeat(32)
    a = np.empty((k // 512, 16))
    for p in range(k // 512):
        a[p, :8] = np.random.permutation(np.resize(levels, 8))
        for g in range(8):
            far = levels[np.abs(levels - a[p, g]) >= 10]
            a[p, g + 8] = far[np.random.randint(len(far))]
    return np.exp2(a.ravel()).repeat(32)


BF16 = ml_dtypes.bfloat16


def bf(x):
    return np.asarray(x, np.float32).astype(BF16)


def f64(x):
    return np.asarray(x).astype(np.float64)


E2M1 = np.array([0.0, 0.5, 1.0, 1.5, 2.0, 3.0, 4.0, 6.0, -0.0, -0.5, -1.0, -1.5, -2.0, -3.0, -4.0, -6.0])


def pack_weight(w, fmt):
    k, n = w.shape
    w = f64(bf(w)).reshape(k // 32, 32, n)
    amax = np.abs(w).max(1)
    if fmt == "e4m3":
        byte = np.frexp(amax)[1] - 1 + 127 - 7
    else:
        mant, ex = np.frexp(amax / 6.0)
        byte = np.where(mant > 0.5, ex, ex - 1) + 127
    byte = np.clip(np.where(amax > 0, byte, 1), 1, 254)
    scaled = (w * np.exp2(127.0 - byte)[:, None, :]).reshape(k, n).astype(np.float32)
    by_word = np.ascontiguousarray(scaled.reshape(k // 512, 128, 4, n).transpose(0, 1, 3, 2))
    if fmt == "e4m3":
        words = by_word.astype(ml_dtypes.float8_e4m3fn).view(np.uint8)
    else:
        c = by_word.astype(ml_dtypes.float4_e2m1fn).view(np.uint8) & 0xF
        words = c[..., 0::2] | (c[..., 1::2] << 4)
    return np.ascontiguousarray(words), np.ascontiguousarray(byte.astype(np.uint8).reshape(k // 512, 16, n))


def unpack_weight(words, scales, fmt):
    g, p, n, _ = words.shape
    if fmt == "e4m3":
        vals = np.ascontiguousarray(words).view(ml_dtypes.float8_e4m3fn).astype(np.float64)
    else:
        nib = np.empty((g, p, n, 4), np.uint8)
        nib[..., 0::2] = words & 0xF
        nib[..., 1::2] = words >> 4
        vals = E2M1[nib]
    vals = vals * np.repeat(np.exp2(scales.astype(np.float64) - 127.0), 8, axis=1)[..., None]
    return vals.transpose(0, 1, 3, 2).reshape(g * 512, n)


B, Q, K, D = 8, 1024, 512, 512
NEG = -10000.0


def draw0():
    s, t = mx_kscale(D), mx_kscale(D)
    query = bf(np.random.standard_normal((B, Q, D)) * s)
    context = bf(np.random.standard_normal((B, K, D)) * 0.5 / t)
    query_bit = bf(np.random.random((B, Q)) > 0.25)
    context_bit = bf(np.random.random((B, K)) > 0.25)
    W_in = np.random.standard_normal((D, D)) * 4.0 / D * t[:, None] / s[None, :]
    words, scales = pack_weight(W_in.T, "e4m3")
    return {"query": query,
            "context": context,
            "query_bit": query_bit,
            "context_bit": context_bit,
            "W_in_words": words,
            "W_in_scales": scales,
            "b_in": bf(np.random.standard_normal(D) / np.sqrt(D) * t)}


def core(query, context, query_bit, context_bit, W_in_words, W_in_scales, b_in):
    ext = (1.0 - f64(query_bit)[:, :, None] * f64(context_bit)[:, None, :]) * NEG
    q = (mxq(f64(query), 2, "e4m3") @ unpack_weight(W_in_words, W_in_scales, "e4m3")) + f64(b_in)
    scores = (mxq(q, 2, "e4m3") @ mxq(f64(context), 2, "e4m3").transpose(0, 2, 1)) + ext
    e = np.exp(scores - scores.max(-1, keepdims=True))
    return e / e.sum(-1, keepdims=True)


def e4m3fn_bytes(y):
    return np.clip(np.asarray(y, np.float64), -448.0, 448.0).astype(np.float32).astype(ml_dtypes.float8_e4m3fn).view(np.uint8)


def e4m3fn_values(b):
    return np.asarray(b, np.uint8).view(ml_dtypes.float8_e4m3fn).astype(np.float64)


def setup_inputs():
    d = draw0()
    x0 = np.asarray(d['query']).astype(np.float64)
    s = (np.max(np.abs(x0), axis=(0, 1), keepdims=True) / 448.0).astype(np.float32)
    out = {}
    for k, v in d.items():
        if k == 'query':
            out['query_bytes'] = e4m3fn_bytes(x0 / s.astype(np.float64))
            out['query_scale'] = s
        else:
            out[k] = v
    return out


def reference(query_bytes, query_scale, context, query_bit, context_bit, W_in_words, W_in_scales, b_in):
    return core(e4m3fn_values(query_bytes) * query_scale.astype(np.float64), context, query_bit, context_bit, W_in_words, W_in_scales, b_in)

@@ -1,0 +1,341 @@
+from contextlib import ExitStack
+
+import concourse.mybir as mybir
+from concourse.masks import make_identity
+
+F32 = mybir.dt.float32
+BF16 = mybir.dt.bfloat16
+I32 = mybir.dt.int32
+U8 = mybir.dt.uint8
+FP8 = mybir.dt.float8_e4m3fn
+FP8X4 = mybir.dt.float8_e4m3fn_x4
+ALU = mybir.AluOpType
+ACT = mybir.ActivationFunctionType
+AX = mybir.AxisListType
+
+B, Q, K, D = 8, 1024, 512, 512
+P = 128
+NEG = 10000.0
+FLOPS = 4 * B * Q * K * D
+BYTES = B * Q * D + 2 * B * K * D + 4 * B * Q * K + D * D + D * D // 32
+
+TILES = 4
+NBLOCKS = B * Q // (P * TILES)
+PER_BATCH = Q // (P * TILES)
+
+
+def tile_attention_pa_t_w8_kernel(
+    tc, query_bytes, query_scale, context, query_bit, context_bit, W_in_words, W_in_scales, b_in, out
+):
+    nc = tc.nc
+    with ExitStack() as ctx:
+        const = ctx.enter_context(tc.tile_pool(name="const", bufs=1))
+        loads = ctx.enter_context(tc.tile_pool(name="loads", bufs=B))
+        work = ctx.enter_context(tc.tile_pool(name="work", bufs=2))
+        psum = ctx.enter_context(tc.psum_pool(name="psum", bufs=2))
+        ctx.enter_context(tc.manual_schedule())
+
+        ident = const.tile([P, P], F32)
+        make_identity(nc, ident[:])
+        warm = const.tile([P, 1], F32)
+        nc.vector.memset(warm[:], 0.0)
+        nc.scalar.activation(out=warm[:], in_=warm[:], func=ACT.Exp)
+        w_scales_raw = const.tile([P, D], U8, align_bytes=64)
+        nc.vector.memset(w_scales_raw[:].bitcast(I32), 0)
+
+        q_in = []
+        c_in = []
+        for b in range(B):
+            bytes_tile = loads.tile([P, 2 * TILES, D], U8, align_bytes=64)
+            rows_tile = loads.tile([P, K // P, D], BF16, align_bytes=64)
+            q_in.append(bytes_tile)
+            c_in.append(rows_tile)
+
+        def load_query(b, lo, hi):
+            src = query_bytes[b].rearrange("(p i) d -> p i d", i=2 * TILES)
+            nc.sync.dma_start(out=q_in[b][:, lo:hi, :], in_=src[:, lo:hi, :])
+
+        def load_context(b, lo, hi):
+            src = context[b].rearrange("(a r) d -> r a d", r=P)
+            nc.sync.dma_start(out=c_in[b][:, lo:hi, :], in_=src[:, lo:hi, :])
+
+        k_scale = const.tile([P, D], F32)
+        w_raw = const.tile([P, D], I32, align_bytes=64)
+        bias_bf = const.tile([P, 4], BF16)
+        qbit_bf = const.tile([P, B, 2 * TILES], BF16)
+        cbit = const.tile([P, B, K], BF16)
+
+        nc.sync.dma_start(out=k_scale[:], in_=query_scale.rearrange("o a k -> (o a k)").partition_broadcast(P))
+        load_query(0, 0, TILES)
+        load_context(0, 0, 2)
+        for quad in range(4):
+            nc.sync.dma_start(
+                out=w_scales_raw[32 * quad : 32 * quad + 4, :].bitcast(I32),
+                in_=W_in_scales[0, 4 * quad : 4 * quad + 4, :].bitcast(I32),
+            )
+        nc.sync.dma_start(out=w_raw[:], in_=W_in_words[0].rearrange("p n t -> p (n t)").bitcast(I32))
+        nc.sync.dma_start(out=bias_bf[:], in_=b_in.rearrange("(p t) -> p t", t=4))
+        load_query(0, TILES, 2 * TILES)
+        load_context(0, 2, 4)
+        nc.sync.dma_start(out=qbit_bf[:], in_=query_bit.rearrange("b (p i) -> p b i", i=2 * TILES))
+        nc.sync.dma_start(
+            out=cbit[:].rearrange("p b j -> p (b j)"), in_=context_bit.rearrange("b j -> (b j)").partition_broadcast(P)
+        )
+        for b in range(1, B):
+            load_query(b, 0, 2 * TILES)
+            load_context(b, 0, 4)
+
+        w_codes = const.tile([P, D], I32, align_bytes=64)
+        w_scales = const.tile([P, D], U8, align_bytes=64)
+        bias = const.tile([P, 4], F32)
+        qbit = const.tile([P, B * 2 * TILES], F32)
+        ncbit = const.tile([P, B, K], BF16)
+
+        def prepare_weights():
+            nc.vector.tensor_copy(
+                out=w_codes[:].rearrange("p (t m) -> p t m", t=4), in_=w_raw[:].rearrange("p (m t) -> p t m", t=4)
+            )
+            nc.vector.tensor_copy(
+                out=w_scales[:].rearrange("p (t m) -> p m t", t=4),
+                in_=w_scales_raw[:].rearrange("p (m t) -> p m t", t=4),
+            )
+            nc.vector.tensor_copy(out=bias[:], in_=bias_bf[:])
+
+        def prepare_masks():
+            nc.vector.tensor_scalar(
+                out=qbit[:],
+                in0=qbit_bf[:].rearrange("p b i -> p (b i)"),
+                scalar1=NEG,
+                scalar2=None,
+                op0=ALU.mult,
+            )
+            for b in range(B):
+                nc.gpsimd.tensor_scalar(
+                    out=ncbit[:, b, :], in0=cbit[:, b, :], scalar1=-1.0, scalar2=1.0, op0=ALU.mult, op1=ALU.add
+                )
+
+        live = {}
+
+        def widen(n):
+            b, h = divmod(n, PER_BATCH)
+            xb = work.tile([P, TILES, D], BF16, align_bytes=64)
+            for j in range(TILES):
+                nc.vector.tensor_tensor(
+                    out=xb[:, j, :],
+                    in0=q_in[b][:, TILES * h + j, :].bitcast(FP8),
+                    in1=k_scale[:],
+                    op=ALU.mult,
+                )
+            live["xb", n] = xb
+
+        def turn(rows, a0):
+            words = rows[:].bitcast(F32)
+            xp = psum.tile([P, 2, 2, P], F32, bufs=2)
+            for a in range(2):
+                for u in range(2):
+                    nc.tensor.transpose(xp[:, a, u, :], words[:, a0 + a, u : D // 2 : 2], ident[:])
+            return xp
+
+        def turn_query(n):
+            xb = live.pop(("xb", n))
+            for half in range(2):
+                live["xp", n, half] = turn(xb, 2 * half)
+
+        def copy_turned(dst, xp):
+            nc.scalar.copy(
+                out=dst.bitcast(F32).rearrange("p (a r u) -> p a r u", a=2, u=2),
+                in_=xp[:].rearrange("p a u r -> p a r u"),
+            )
+
+        def copy_query(n):
+            xt = work.tile([P, TILES * P * 4], BF16, align_bytes=64)
+            for half in range(2):
+                xp = live.pop(("xp", n, half))
+                copy_turned(xt[:, 1024 * half : 1024 * (half + 1)], xp)
+            live["xt", n] = xt
+
+        def quantize_query(n):
+            xt = live.pop(("xt", n))
+            xc = work.tile([P, TILES * P], I32, align_bytes=64)
+            xs = work.tile([P, TILES * P], U8, align_bytes=64)
+            nc.vector.quantize_mx(out=xc[:].bitcast(FP8X4), scales=xs[:], in_=xt[:])
+            live["xq", n] = (xc, xs)
+
+        def project(n, t):
+            xc, xs = live["xq", n]
+            qm = psum.tile([P, TILES * P], F32, bufs=3)
+            nc.tensor.matmul_mx(
+                out=qm[:],
+                lhsT=w_codes[:, P * t : P * (t + 1)].bitcast(FP8X4),
+                lhsT_scale=w_scales[:, P * t : P * (t + 1)],
+                rhs=xc[:].bitcast(FP8X4),
+                rhs_scale=xs[:],
+                start=True,
+                stop=True,
+            )
+            live["qm", n, t] = qm
+
+        def add_bias(n, t):
+            if t == 0:
+                qp = work.tile([P, 4, TILES * P], BF16, align_bytes=64)
+                live["qp", n] = qp
+            qm = live.pop(("qm", n, t))
+            nc.scalar.activation(
+                out=live["qp", n][:, t, :], in_=qm[:], func=ACT.Identity, bias=bias[:, t : t + 1]
+            )
+
+        def interleave(n):
+            qp = live.pop(("qp", n))
+            qi = work.tile([P, TILES * P, 4], BF16, align_bytes=64)
+            for j in range(TILES):
+                cols = slice(P * j, P * (j + 1))
+                nc.gpsimd.tensor_scalar(
+                    out=qi[:, cols, :],
+                    in0=qp[:, :, cols].rearrange("p t c -> p c t"),
+                    scalar1=1.0,
+                    scalar2=0.0,
+                    op0=ALU.mult,
+                    op1=ALU.add,
+                )
+            live["qi", n] = qi
+
+        def quantize_q(n):
+            qi = live.pop(("qi", n))
+            qc = work.tile([P, TILES * P], I32, align_bytes=64)
+            qs = work.tile([P, TILES * P], U8, align_bytes=64)
+            nc.vector.quantize_mx(
+                out=qc[:].bitcast(FP8X4), scales=qs[:], in_=qi[:].rearrange("p c t -> p (c t)")
+            )
+            live["qq", n] = (qc, qs)
+
+        def score(n, j):
+            qc, qs = live["qq", n]
+            cc, cs = live["cq", n // PER_BATCH]
+            sm = psum.tile([P, K], F32, bufs=3)
+            nc.tensor.matmul_mx(
+                out=sm[:],
+                lhsT=qc[:, P * j : P * (j + 1)].bitcast(FP8X4),
+                lhsT_scale=qs[:, P * j : P * (j + 1)],
+                rhs=cc[:].bitcast(FP8X4),
+                rhs_scale=cs[:],
+                start=True,
+                stop=True,
+            )
+            live["sm", n, j] = sm
+
+        def mask(n, j):
+            b, h = divmod(n, PER_BATCH)
+            if j == 0:
+                y = work.tile([P, TILES, K], F32, bufs=4)
+                live["y", n] = y
+            sm = live.pop(("sm", n, j))
+            column = b * 2 * TILES + TILES * h + j
+            nc.vector.scalar_tensor_tensor(
+                out=live["y", n][:, j, :],
+                in0=ncbit[:, b, :],
+                scalar=qbit[:, column : column + 1],
+                in1=sm[:],
+                op0=ALU.mult,
+                op1=ALU.subtract,
+            )
+
+        def row_min(n):
+            ymin = work.tile([P, TILES], F32, bufs=3)
+            nc.vector.tensor_reduce(out=ymin[:], in_=live["y", n][:], axis=AX.X, op=ALU.min)
+            live["ymin", n] = ymin
+
+        def exponent(n):
+            y = live["y", n]
+            ymin = live.pop(("ymin", n))
+            z = work.tile([P, TILES], F32, bufs=3)
+            for j in range(TILES):
+                nc.scalar.activation(
+                    out=y[:, j, :],
+                    in_=y[:, j, :],
+                    func=ACT.Exp,
+                    bias=ymin[:, j : j + 1],
+                    scale=-1.0,
+                    accum_out=z[:, j : j + 1],
+                )
+            live["z", n] = z
+
+        def invert(n):
+            rz = work.tile([P, TILES], F32, bufs=3)
+            nc.vector.reciprocal(out=rz[:], in_=live.pop(("z", n))[:])
+            live["rz", n] = rz
+
+        def normalize(n):
+            y = live.pop(("y", n))
+            rz = live.pop(("rz", n))
+            b, h = divmod(n, PER_BATCH)
+            for j in range(TILES):
+                nc.scalar.activation(out=y[:, j, :], in_=y[:, j, :], func=ACT.Copy, scale=rz[:, j : j + 1])
+            dst = out[b].rearrange("(p i) j -> p i j", i=2 * TILES)
+            nc.sync.dma_start(out=dst[:, TILES * h : TILES * (h + 1), :], in_=y[:])
+
+        def turn_context(m):
+            b, h = divmod(m, 2)
+            live["cp", m] = turn(c_in[b], 2 * h)
+
+        def copy_context(m):
+            ct = work.tile([P, 2 * P * 4], BF16, align_bytes=64)
+            copy_turned(ct[:], live.pop(("cp", m)))
+            live["ct", m] = ct
+
+        def quantize_context(m):
+            b, h = divmod(m, 2)
+            if h == 0:
+                cc = work.tile([P, K], I32, align_bytes=64, bufs=3)
+                cs = work.tile([P, K], U8, align_bytes=64, bufs=3)
+                live["cq", b] = (cc, cs)
+            cc, cs = live["cq", b]
+            ct = live.pop(("ct", m))
+            cols = slice(2 * P * h, 2 * P * (h + 1))
+            nc.vector.quantize_mx(out=cc[:, cols].bitcast(FP8X4), scales=cs[:, cols], in_=ct[:])
+
+        def real(n):
+            return 0 <= n < NBLOCKS
+
+        for i in range(-3, NBLOCKS + 1):
+            if real(i - 1):
+                exponent(i - 1)
+            if real(i + 1):
+                for t in range(3):
+                    project(i + 1, t)
+            if real(i + 3):
+                widen(i + 3)
+                turn_query(i + 3)
+            if i == -2:
+                prepare_weights()
+            if real(i):
+                quantize_q(i)
+                for j in range(3):
+                    score(i, j)
+            if real(i + 1):
+                add_bias(i + 1, 0)
+                project(i + 1, 3)
+                for t in range(1, 4):
+                    add_bias(i + 1, t)
+            if i == -1:
+                prepare_masks()
+            if real(i + 2):
+                quantize_query(i + 2)
+                quantize_context(i + 2)
+            if real(i + 1):
+                interleave(i + 1)
+            if real(i):
+                mask(i, 0)
+                score(i, 3)
+                for j in range(1, 4):
+                    mask(i, j)
+            if real(i - 1):
+                invert(i - 1)
+            if real(i):
+                row_min(i)
+            if real(i + 3):
+                copy_query(i + 3)
+                turn_context(i + 3)
+            if real(i - 1):
+                normalize(i - 1)
+            if real(i + 3):
+                copy_context(i + 3)

@@ -22,6 +22,8 @@ BYTES = B * Q * D + 2 * B * K * D + 4 * B * Q * K + D * D + D * D // 32
 TILES = 4
 NBLOCKS = B * Q // (P * TILES)
 PER_BATCH = Q // (P * TILES)
+I_SPLIT = [320] * NBLOCKS
+NORM = [["scalar"] * 4 for n in range(NBLOCKS - 2)] + [["vector"] * 4] * 2
 
 
 def tile_attention_pa_t_w8_kernel(
@@ -65,25 +67,30 @@ def tile_attention_pa_t_w8_kernel(
         qbit_bf = const.tile([P, B, 2 * TILES], BF16)
         cbit = const.tile([P, B, K], BF16)
 
+        def load_context_bits(b):
+            nc.sync.dma_start(out=cbit[:, b, :], in_=context_bit[b].partition_broadcast(P))
+
         nc.sync.dma_start(out=k_scale[:], in_=query_scale.rearrange("o a k -> (o a k)").partition_broadcast(P))
         load_query(0, 0, TILES)
         load_context(0, 0, 2)
+        load_query(0, TILES, 2 * TILES)
+        nc.sync.dma_start(out=w_raw[:], in_=W_in_words[0].rearrange("p n t -> p (n t)").bitcast(I32))
         for quad in range(4):
             nc.sync.dma_start(
                 out=w_scales_raw[32 * quad : 32 * quad + 4, :].bitcast(I32),
                 in_=W_in_scales[0, 4 * quad : 4 * quad + 4, :].bitcast(I32),
             )
-        nc.sync.dma_start(out=w_raw[:], in_=W_in_words[0].rearrange("p n t -> p (n t)").bitcast(I32))
-        nc.sync.dma_start(out=bias_bf[:], in_=b_in.rearrange("(p t) -> p t", t=4))
-        load_query(0, TILES, 2 * TILES)
         load_context(0, 2, 4)
-        nc.sync.dma_start(out=qbit_bf[:], in_=query_bit.rearrange("b (p i) -> p b i", i=2 * TILES))
-        nc.sync.dma_start(
-            out=cbit[:].rearrange("p b j -> p (b j)"), in_=context_bit.rearrange("b j -> (b j)").partition_broadcast(P)
-        )
-        for b in range(1, B):
+        load_query(1, 0, 2 * TILES)
+        load_context(1, 0, 4)
+        load_context_bits(1)
+        nc.gpsimd.dma_start(out=bias_bf[:], in_=b_in.rearrange("(p t) -> p t", t=4))
+        nc.gpsimd.dma_start(out=qbit_bf[:], in_=query_bit.rearrange("b (p i) -> p b i", i=2 * TILES))
+        nc.gpsimd.dma_start(out=cbit[:, 0, :], in_=context_bit[0].partition_broadcast(P))
+        for b in range(2, B):
             load_query(b, 0, 2 * TILES)
             load_context(b, 0, 4)
+            load_context_bits(b)
 
         w_codes = const.tile([P, D], I32, align_bytes=64)
         w_scales = const.tile([P, D], U8, align_bytes=64)
@@ -101,7 +108,7 @@ def tile_attention_pa_t_w8_kernel(
             )
             nc.vector.tensor_copy(out=bias[:], in_=bias_bf[:])
 
-        def prepare_masks():
+        def prepare_query_bits():
             nc.vector.tensor_scalar(
                 out=qbit[:],
                 in0=qbit_bf[:].rearrange("p b i -> p (b i)"),
@@ -109,10 +116,11 @@ def tile_attention_pa_t_w8_kernel(
                 scalar2=None,
                 op0=ALU.mult,
             )
-            for b in range(B):
-                nc.gpsimd.tensor_scalar(
-                    out=ncbit[:, b, :], in0=cbit[:, b, :], scalar1=-1.0, scalar2=1.0, op0=ALU.mult, op1=ALU.add
-                )
+
+        def prepare_context_bits(b):
+            nc.vector.tensor_scalar(
+                out=ncbit[:, b, :], in0=cbit[:, b, :], scalar1=-1.0, scalar2=1.0, op0=ALU.mult, op1=ALU.add
+            )
 
         live = {}
 
@@ -184,20 +192,21 @@ def tile_attention_pa_t_w8_kernel(
                 out=live["qp", n][:, t, :], in_=qm[:], func=ACT.Identity, bias=bias[:, t : t + 1]
             )
 
-        def interleave(n):
-            qp = live.pop(("qp", n))
+        def split(n):
+            return I_SPLIT[n]
+
+        def interleave_scalar(n):
             qi = work.tile([P, TILES * P, 4], BF16, align_bytes=64)
-            for j in range(TILES):
-                cols = slice(P * j, P * (j + 1))
-                nc.gpsimd.tensor_scalar(
-                    out=qi[:, cols, :],
-                    in0=qp[:, :, cols].rearrange("p t c -> p c t"),
-                    scalar1=1.0,
-                    scalar2=0.0,
-                    op0=ALU.mult,
-                    op1=ALU.add,
-                )
             live["qi", n] = qi
+            cols = slice(split(n), TILES * P)
+            if split(n) < TILES * P:
+                nc.scalar.copy(out=qi[:, cols, :], in_=live["qp", n][:, :, cols].rearrange("p t c -> p c t"))
+
+        def interleave_vector(n):
+            qp = live.pop(("qp", n))
+            cols = slice(0, split(n))
+            if split(n) > 0:
+                nc.vector.tensor_copy(out=live["qi", n][:, cols, :], in_=qp[:, :, cols].rearrange("p t c -> p c t"))
 
         def quantize_q(n):
             qi = live.pop(("qi", n))
@@ -239,39 +248,50 @@ def tile_attention_pa_t_w8_kernel(
                 op1=ALU.subtract,
             )
 
-        def row_min(n):
-            ymin = work.tile([P, TILES], F32, bufs=3)
-            nc.vector.tensor_reduce(out=ymin[:], in_=live["y", n][:], axis=AX.X, op=ALU.min)
-            live["ymin", n] = ymin
+        def row_min(n, js):
+            if js.start == 0:
+                ymin = work.tile([P, TILES], F32, bufs=3)
+                live["ymin", n] = ymin
+            nc.vector.tensor_reduce(out=live["ymin", n][:, js], in_=live["y", n][:, js, :], axis=AX.X, op=ALU.min)
 
-        def exponent(n):
+        def exponent(n, js):
             y = live["y", n]
-            ymin = live.pop(("ymin", n))
-            z = work.tile([P, TILES], F32, bufs=3)
-            for j in range(TILES):
+            if js.start == 0:
+                z = work.tile([P, TILES], F32, bufs=3)
+                live["z", n] = z
+            for j in range(js.start, js.stop):
                 nc.scalar.activation(
                     out=y[:, j, :],
                     in_=y[:, j, :],
                     func=ACT.Exp,
-                    bias=ymin[:, j : j + 1],
+                    bias=live["ymin", n][:, j : j + 1],
                     scale=-1.0,
-                    accum_out=z[:, j : j + 1],
+                    accum_out=live["z", n][:, j : j + 1],
                 )
-            live["z", n] = z
 
-        def invert(n):
-            rz = work.tile([P, TILES], F32, bufs=3)
-            nc.vector.reciprocal(out=rz[:], in_=live.pop(("z", n))[:])
-            live["rz", n] = rz
+        def invert(n, js):
+            if js.start == 0:
+                rz = work.tile([P, TILES], F32, bufs=3)
+                live["rz", n] = rz
+            nc.vector.reciprocal(out=live["rz", n][:, js], in_=live["z", n][:, js])
 
-        def normalize(n):
-            y = live.pop(("y", n))
-            rz = live.pop(("rz", n))
+        def normalize(n, js, engine):
+            y = live["y", n]
+            rz = live["rz", n]
+            for j in range(js.start, js.stop):
+                if engine == "scalar":
+                    nc.scalar.activation(out=y[:, j, :], in_=y[:, j, :], func=ACT.Copy, scale=rz[:, j : j + 1])
+                else:
+                    nc.vector.tensor_scalar(
+                        out=y[:, j, :], in0=y[:, j, :], scalar1=rz[:, j : j + 1], scalar2=None, op0=ALU.mult
+                    )
+
+        def store(n, js):
             b, h = divmod(n, PER_BATCH)
-            for j in range(TILES):
-                nc.scalar.activation(out=y[:, j, :], in_=y[:, j, :], func=ACT.Copy, scale=rz[:, j : j + 1])
             dst = out[b].rearrange("(p i) j -> p i j", i=2 * TILES)
-            nc.sync.dma_start(out=dst[:, TILES * h : TILES * (h + 1), :], in_=y[:])
+            nc.sync.dma_start(
+                out=dst[:, TILES * h + js.start : TILES * h + js.stop, :], in_=live["y", n][:, js, :]
+            )
 
         def turn_context(m):
             b, h = divmod(m, 2)
@@ -296,9 +316,11 @@ def tile_attention_pa_t_w8_kernel(
         def real(n):
             return 0 <= n < NBLOCKS
 
+        every = slice(0, TILES)
+        last = NBLOCKS - 1
         for i in range(-3, NBLOCKS + 1):
-            if real(i - 1):
-                exponent(i - 1)
+            if real(i - 1) and i - 1 != last:
+                exponent(i - 1, every)
             if real(i + 1):
                 for t in range(3):
                     project(i + 1, t)
@@ -307,6 +329,8 @@ def tile_attention_pa_t_w8_kernel(
                 turn_query(i + 3)
             if i == -2:
                 prepare_weights()
+            if i == -1:
+                prepare_query_bits()
             if real(i):
                 quantize_q(i)
                 for j in range(3):
@@ -316,26 +340,43 @@ def tile_attention_pa_t_w8_kernel(
                 project(i + 1, 3)
                 for t in range(1, 4):
                     add_bias(i + 1, t)
-            if i == -1:
-                prepare_masks()
+                interleave_scalar(i + 1)
             if real(i + 2):
                 quantize_query(i + 2)
                 quantize_context(i + 2)
-            if real(i + 1):
-                interleave(i + 1)
+            if real(i + 1) and (i + 1) % PER_BATCH == 0:
+                prepare_context_bits((i + 1) // PER_BATCH)
             if real(i):
                 mask(i, 0)
                 score(i, 3)
-                for j in range(1, 4):
-                    mask(i, j)
-            if real(i - 1):
-                invert(i - 1)
-            if real(i):
-                row_min(i)
+                if i != last:
+                    for j in range(1, 4):
+                        mask(i, j)
+                else:
+                    for j in range(TILES):
+                        js = slice(j, j + 1)
+                        row_min(i, js)
+                        exponent(i, js)
+                        if j + 1 < TILES:
+                            mask(i, j + 1)
+            if real(i - 1) and i - 1 != last:
+                invert(i - 1, every)
+            if real(i) and i != last:
+                row_min(i, every)
+            if real(i + 1):
+                interleave_vector(i + 1)
             if real(i + 3):
                 copy_query(i + 3)
                 turn_context(i + 3)
-            if real(i - 1):
-                normalize(i - 1)
+            if real(i - 1) and i - 1 != last:
+                for j in range(TILES):
+                    normalize(i - 1, slice(j, j + 1), NORM[i - 1][j])
+                store(i - 1, every)
+            if i == last:
+                for j in range(TILES):
+                    js = slice(j, j + 1)
+                    invert(i, js)
+                    normalize(i, js, NORM[i][j])
+                    store(i, js)
             if real(i + 3):
                 copy_context(i + 3)

@@ -22,8 +22,8 @@ BYTES = B * Q * D + 2 * B * K * D + 4 * B * Q * K + D * D + D * D // 32
 TILES = 4
 NBLOCKS = B * Q // (P * TILES)
 PER_BATCH = Q // (P * TILES)
-I_SPLIT = [320] * NBLOCKS
-NORM = [["scalar"] * 4 for n in range(NBLOCKS - 2)] + [["vector"] * 4] * 2
+INTER = [["vector", "vector", "vector", "scalar"]] + [["gpsimd"] * 4] * (NBLOCKS - 2) + [["vector", "vector", "vector", "scalar"]]
+NORM = [["vector", "scalar", "scalar", "scalar"], ["scalar"] * 4] * (NBLOCKS // 2 - 1) + [["vector", "scalar"] * 2] * 2
 
 
 def tile_attention_pa_t_w8_kernel(
@@ -61,7 +61,7 @@ def tile_attention_pa_t_w8_kernel(
             src = context[b].rearrange("(a r) d -> r a d", r=P)
             nc.sync.dma_start(out=c_in[b][:, lo:hi, :], in_=src[:, lo:hi, :])
 
-        k_scale = const.tile([P, D], F32)
+        k_scale = const.tile([P, 4], F32)
         w_raw = const.tile([P, D], I32, align_bytes=64)
         bias_bf = const.tile([P, 4], BF16)
         qbit_bf = const.tile([P, B, 2 * TILES], BF16)
@@ -70,17 +70,16 @@ def tile_attention_pa_t_w8_kernel(
         def load_context_bits(b):
             nc.sync.dma_start(out=cbit[:, b, :], in_=context_bit[b].partition_broadcast(P))
 
-        nc.sync.dma_start(out=k_scale[:], in_=query_scale.rearrange("o a k -> (o a k)").partition_broadcast(P))
         load_query(0, 0, TILES)
-        load_context(0, 0, 2)
-        load_query(0, TILES, 2 * TILES)
+        nc.sync.dma_start(out=k_scale[:], in_=query_scale.rearrange("o a (p t) -> p (o a t)", t=4))
         nc.sync.dma_start(out=w_raw[:], in_=W_in_words[0].rearrange("p n t -> p (n t)").bitcast(I32))
         for quad in range(4):
             nc.sync.dma_start(
                 out=w_scales_raw[32 * quad : 32 * quad + 4, :].bitcast(I32),
                 in_=W_in_scales[0, 4 * quad : 4 * quad + 4, :].bitcast(I32),
             )
-        load_context(0, 2, 4)
+        load_query(0, TILES, 2 * TILES)
+        load_context(0, 0, 4)
         load_query(1, 0, 2 * TILES)
         load_context(1, 0, 4)
         load_context_bits(1)
@@ -124,54 +123,51 @@ def tile_attention_pa_t_w8_kernel(
 
         live = {}
 
-        def widen(n):
+        def widen(n, half, halves=1):
             b, h = divmod(n, PER_BATCH)
-            xb = work.tile([P, TILES, D], BF16, align_bytes=64)
-            for j in range(TILES):
-                nc.vector.tensor_tensor(
-                    out=xb[:, j, :],
-                    in0=q_in[b][:, TILES * h + j, :].bitcast(FP8),
-                    in1=k_scale[:],
-                    op=ALU.mult,
-                )
-            live["xb", n] = xb
-
-        def turn(rows, a0):
-            words = rows[:].bitcast(F32)
-            xp = psum.tile([P, 2, 2, P], F32, bufs=2)
-            for a in range(2):
-                for u in range(2):
-                    nc.tensor.transpose(xp[:, a, u, :], words[:, a0 + a, u : D // 2 : 2], ident[:])
-            return xp
-
-        def turn_query(n):
-            xb = live.pop(("xb", n))
-            for half in range(2):
-                live["xp", n, half] = turn(xb, 2 * half)
-
-        def copy_turned(dst, xp):
+            if half == 0:
+                xb = work.tile([P, TILES, D], BF16, align_bytes=64)
+                live["xb", n] = xb
+            js = slice(2 * half, 2 * (half + halves))
+            src = slice(TILES * h + 2 * half, TILES * h + 2 * (half + halves))
             nc.scalar.copy(
-                out=dst.bitcast(F32).rearrange("p (a r u) -> p a r u", a=2, u=2),
-                in_=xp[:].rearrange("p a u r -> p a r u"),
+                out=live["xb", n][:, js, :].rearrange("p i d -> p (i d)"),
+                in_=q_in[b][:, src, :].rearrange("p i d -> p (i d)").bitcast(FP8),
             )
 
-        def copy_query(n):
-            xt = work.tile([P, TILES * P * 4], BF16, align_bytes=64)
-            for half in range(2):
-                xp = live.pop(("xp", n, half))
-                copy_turned(xt[:, 1024 * half : 1024 * (half + 1)], xp)
-            live["xt", n] = xt
+        def turn(rows, a0, tag):
+            words = rows[:].bitcast(F32)
+            xp = psum.tile([P, 2, 2, P], F32, tag=tag, bufs=1)
+            for a in range(2):
+                for u in range(2):
+                    nc.tensor.transpose(xp[:, u, a, :], words[:, a0 + a, u : D // 2 : 2], ident[:])
+            return xp
+
+        def turn_query(n, half):
+            live["xp", n, half] = turn(live["xb", n], 2 * half, "xp%d" % half)
+
+        def scale_query(n, half):
+            if half == 0:
+                xt = work.tile([P, TILES * P, 4], BF16, align_bytes=64)
+                live["xt", n] = xt
+            xp = live.pop(("xp", n, half))
+            nc.vector.tensor_tensor(
+                out=live["xt", n][:, 256 * half : 256 * (half + 1), :].rearrange("p c (u e) -> p c u e", u=2),
+                in0=xp[:].bitcast(BF16).rearrange("p u a (r e) -> p (a r) u e", e=2),
+                in1=k_scale[:].rearrange("p (u e) -> p u e", u=2).unsqueeze(1).to_broadcast([P, 256, 2, 2]),
+                op=ALU.mult,
+            )
 
         def quantize_query(n):
             xt = live.pop(("xt", n))
             xc = work.tile([P, TILES * P], I32, align_bytes=64)
             xs = work.tile([P, TILES * P], U8, align_bytes=64)
-            nc.vector.quantize_mx(out=xc[:].bitcast(FP8X4), scales=xs[:], in_=xt[:])
+            nc.vector.quantize_mx(out=xc[:].bitcast(FP8X4), scales=xs[:], in_=xt[:].rearrange("p c t -> p (c t)"))
             live["xq", n] = (xc, xs)
 
         def project(n, t):
             xc, xs = live["xq", n]
-            qm = psum.tile([P, TILES * P], F32, bufs=3)
+            qm = psum.tile([P, TILES * P], F32, bufs=2)
             nc.tensor.matmul_mx(
                 out=qm[:],
                 lhsT=w_codes[:, P * t : P * (t + 1)].bitcast(FP8X4),
@@ -192,21 +188,21 @@ def tile_attention_pa_t_w8_kernel(
                 out=live["qp", n][:, t, :], in_=qm[:], func=ACT.Identity, bias=bias[:, t : t + 1]
             )
 
-        def split(n):
-            return I_SPLIT[n]
-
-        def interleave_scalar(n):
-            qi = work.tile([P, TILES * P, 4], BF16, align_bytes=64)
-            live["qi", n] = qi
-            cols = slice(split(n), TILES * P)
-            if split(n) < TILES * P:
-                nc.scalar.copy(out=qi[:, cols, :], in_=live["qp", n][:, :, cols].rearrange("p t c -> p c t"))
-
-        def interleave_vector(n):
-            qp = live.pop(("qp", n))
-            cols = slice(0, split(n))
-            if split(n) > 0:
-                nc.vector.tensor_copy(out=live["qi", n][:, cols, :], in_=qp[:, :, cols].rearrange("p t c -> p c t"))
+        def interleave(n, chunk, engine):
+            if chunk == 0:
+                qi = work.tile([P, TILES * P, 4], BF16, align_bytes=64)
+                live["qi", n] = qi
+            cols = slice(P * chunk, P * (chunk + 1))
+            dst = live["qi", n][:, cols, :]
+            rows = live["qp", n][:, :, cols].rearrange("p t c -> p c t")
+            if engine == "gpsimd":
+                nc.gpsimd.tensor_scalar(
+                    out=dst, in0=rows, scalar1=1.0, scalar2=0.0, op0=ALU.mult, op1=ALU.add
+                )
+            elif engine == "vector":
+                nc.vector.tensor_copy(out=dst, in_=rows)
+            else:
+                nc.scalar.copy(out=dst, in_=rows)
 
         def quantize_q(n):
             qi = live.pop(("qi", n))
@@ -295,11 +291,14 @@ def tile_attention_pa_t_w8_kernel(
 
         def turn_context(m):
             b, h = divmod(m, 2)
-            live["cp", m] = turn(c_in[b], 2 * h)
+            live["cp", m] = turn(c_in[b], 2 * h, "cp")
 
         def copy_context(m):
             ct = work.tile([P, 2 * P * 4], BF16, align_bytes=64)
-            copy_turned(ct[:], live.pop(("cp", m)))
+            nc.scalar.copy(
+                out=ct[:].bitcast(F32).rearrange("p (c u) -> p c u", u=2),
+                in_=live.pop(("cp", m))[:].rearrange("p u a r -> p (a r) u"),
+            )
             live["ct", m] = ct
 
         def quantize_context(m):
@@ -318,65 +317,113 @@ def tile_attention_pa_t_w8_kernel(
 
         every = slice(0, TILES)
         last = NBLOCKS - 1
-        for i in range(-3, NBLOCKS + 1):
-            if real(i - 1) and i - 1 != last:
-                exponent(i - 1, every)
-            if real(i + 1):
-                for t in range(3):
-                    project(i + 1, t)
-            if real(i + 3):
-                widen(i + 3)
-                turn_query(i + 3)
-            if i == -2:
-                prepare_weights()
-            if i == -1:
-                prepare_query_bits()
-            if real(i):
-                quantize_q(i)
-                for j in range(3):
-                    score(i, j)
+
+        for half in range(2):
+            widen(0, half)
+            turn_query(0, half)
+            scale_query(0, half)
+        widen(1, 0, 2)
+        turn_context(0)
+        copy_context(0)
+        prepare_weights()
+        quantize_query(0)
+        turn_query(1, 0)
+        scale_query(1, 0)
+        for t in range(2):
+            project(0, t)
+        turn_query(1, 1)
+        scale_query(1, 1)
+        turn_context(1)
+        add_bias(0, 0)
+        project(0, 2)
+        add_bias(0, 1)
+        project(0, 3)
+        copy_context(1)
+        quantize_context(0)
+        quantize_query(1)
+        add_bias(0, 2)
+        add_bias(0, 3)
+        for t in range(2):
+            project(1, t)
+        quantize_context(1)
+        for chunk in range(4):
+            interleave(0, chunk, INTER[0][chunk])
+        prepare_query_bits()
+        prepare_context_bits(0)
+
+        for i in range(NBLOCKS):
             if real(i + 1):
                 add_bias(i + 1, 0)
-                project(i + 1, 3)
-                for t in range(1, 4):
-                    add_bias(i + 1, t)
-                interleave_scalar(i + 1)
-            if real(i + 2):
-                quantize_query(i + 2)
-                quantize_context(i + 2)
-            if real(i + 1) and (i + 1) % PER_BATCH == 0:
-                prepare_context_bits((i + 1) // PER_BATCH)
-            if real(i):
-                mask(i, 0)
-                score(i, 3)
-                if i != last:
-                    for j in range(1, 4):
-                        mask(i, j)
-                else:
-                    for j in range(TILES):
-                        js = slice(j, j + 1)
-                        row_min(i, js)
-                        exponent(i, js)
-                        if j + 1 < TILES:
-                            mask(i, j + 1)
-            if real(i - 1) and i - 1 != last:
-                invert(i - 1, every)
-            if real(i) and i != last:
-                row_min(i, every)
+                project(i + 1, 2)
+                add_bias(i + 1, 1)
+            quantize_q(i)
+            for j in range(3):
+                score(i, j)
             if real(i + 1):
-                interleave_vector(i + 1)
-            if real(i + 3):
-                copy_query(i + 3)
-                turn_context(i + 3)
-            if real(i - 1) and i - 1 != last:
-                for j in range(TILES):
-                    normalize(i - 1, slice(j, j + 1), NORM[i - 1][j])
-                store(i - 1, every)
+                project(i + 1, 3)
+                add_bias(i + 1, 2)
+                add_bias(i + 1, 3)
+                if i + 1 != last:
+                    for chunk in range(4):
+                        interleave(i + 1, chunk, INTER[i + 1][chunk])
+                if (i + 1) % PER_BATCH == 0:
+                    prepare_context_bits((i + 1) // PER_BATCH)
+            if i > 0 and real(i + 2):
+                if i == 1:
+                    quantize_context(2)
+                quantize_context(i + 2)
             if i == last:
+                exponent(i - 1, every)
+            mask(i, 0)
+            score(i, 3)
+            if i == 0:
+                widen(2, 0, 2)
+                for half in range(2):
+                    turn_query(2, half)
+                turn_context(2)
+                copy_context(2)
+            if i == last:
+                for j in range(TILES):
+                    js = slice(j, j + 1)
+                    row_min(i, js)
+                    if j == 2:
+                        invert(i - 1, every)
+                        for jj in range(TILES):
+                            normalize(i - 1, slice(jj, jj + 1), NORM[i - 1][jj])
+                        store(i - 1, every)
+                    exponent(i, js)
+                    if j + 1 < TILES:
+                        mask(i, j + 1)
                 for j in range(TILES):
                     js = slice(j, j + 1)
                     invert(i, js)
                     normalize(i, js, NORM[i][j])
                     store(i, js)
+                break
+            for j in range(1, 4):
+                mask(i, j)
+            if real(i + 2):
+                scale_query(i + 2, 0)
+                scale_query(i + 2, 1)
             if real(i + 3):
+                turn_context(i + 3)
+            if real(i - 1):
+                exponent(i - 1, every)
+                invert(i - 1, every)
+            if real(i + 2):
+                quantize_query(i + 2)
+                for t in range(2):
+                    project(i + 2, t)
+            row_min(i, every)
+            if i + 1 == last:
+                for chunk in range(4):
+                    interleave(last, chunk, INTER[last][chunk])
+            if real(i + 3):
+                widen(i + 3, 0, 2)
                 copy_context(i + 3)
+                for half in range(2):
+                    turn_query(i + 3, half)
+            if real(i - 1):
+                for j in range(TILES):
+                    normalize(i - 1, slice(j, j + 1), NORM[i - 1][j])
+                store(i - 1, every)

@@ -22,8 +22,19 @@ BYTES = B * Q * D + 2 * B * K * D + 4 * B * Q * K + D * D + D * D // 32
 TILES = 4
 NBLOCKS = B * Q // (P * TILES)
 PER_BATCH = Q // (P * TILES)
-INTER = [["vector", "vector", "vector", "scalar"]] + [["gpsimd"] * 4] * (NBLOCKS - 2) + [["vector", "vector", "vector", "scalar"]]
-NORM = [["vector", "scalar", "scalar", "scalar"], ["scalar"] * 4] * (NBLOCKS // 2 - 1) + [["vector", "scalar"] * 2] * 2
+INTER = (
+    [["vector", "vector", "vector", "scalar"]]
+    + [["gpsimd"] * 4] * (NBLOCKS - 3)
+    + [["gpsimd", "gpsimd", "gpsimd", "scalar"]]
+    + [["vector", "vector", "vector", "scalar"]]
+)
+NORM = (
+    [["gpsimd", "scalar", "scalar", "scalar"]] * (NBLOCKS - 5)
+    + [["scalar", "scalar", "scalar", "vector"]] * 2
+    + [["scalar", "vector"] * 2]
+    + [["scalar"] * 4]
+    + [["scalar", "vector", "vector", "vector"]]
+)
 
 
 def tile_attention_pa_t_w8_kernel(
@@ -70,15 +81,16 @@ def tile_attention_pa_t_w8_kernel(
         def load_context_bits(b):
             nc.sync.dma_start(out=cbit[:, b, :], in_=context_bit[b].partition_broadcast(P))
 
-        load_query(0, 0, TILES)
+        load_query(0, 0, 2)
+        load_query(0, 2, TILES)
         nc.sync.dma_start(out=k_scale[:], in_=query_scale.rearrange("o a (p t) -> p (o a t)", t=4))
+        load_query(0, TILES, 2 * TILES)
         nc.sync.dma_start(out=w_raw[:], in_=W_in_words[0].rearrange("p n t -> p (n t)").bitcast(I32))
         for quad in range(4):
             nc.sync.dma_start(
                 out=w_scales_raw[32 * quad : 32 * quad + 4, :].bitcast(I32),
                 in_=W_in_scales[0, 4 * quad : 4 * quad + 4, :].bitcast(I32),
             )
-        load_query(0, TILES, 2 * TILES)
         load_context(0, 0, 4)
         load_query(1, 0, 2 * TILES)
         load_context(1, 0, 4)
@@ -190,7 +202,7 @@ def tile_attention_pa_t_w8_kernel(
 
         def interleave(n, chunk, engine):
             if chunk == 0:
-                qi = work.tile([P, TILES * P, 4], BF16, align_bytes=64)
+                qi = work.tile([P, TILES * P, 4], BF16, align_bytes=64, bufs=1)
                 live["qi", n] = qi
             cols = slice(P * chunk, P * (chunk + 1))
             dst = live["qi", n][:, cols, :]
@@ -231,7 +243,7 @@ def tile_attention_pa_t_w8_kernel(
         def mask(n, j):
             b, h = divmod(n, PER_BATCH)
             if j == 0:
-                y = work.tile([P, TILES, K], F32, bufs=4)
+                y = work.tile([P, TILES, K], F32, bufs=5)
                 live["y", n] = y
             sm = live.pop(("sm", n, j))
             column = b * 2 * TILES + TILES * h + j
@@ -267,7 +279,7 @@ def tile_attention_pa_t_w8_kernel(
 
         def invert(n, js):
             if js.start == 0:
-                rz = work.tile([P, TILES], F32, bufs=3)
+                rz = work.tile([P, TILES], F32, bufs=4)
                 live["rz", n] = rz
             nc.vector.reciprocal(out=live["rz", n][:, js], in_=live["z", n][:, js])
 
@@ -277,9 +289,18 @@ def tile_attention_pa_t_w8_kernel(
             for j in range(js.start, js.stop):
                 if engine == "scalar":
                     nc.scalar.activation(out=y[:, j, :], in_=y[:, j, :], func=ACT.Copy, scale=rz[:, j : j + 1])
-                else:
+                elif engine == "vector":
                     nc.vector.tensor_scalar(
                         out=y[:, j, :], in0=y[:, j, :], scalar1=rz[:, j : j + 1], scalar2=None, op0=ALU.mult
+                    )
+                else:
+                    nc.gpsimd.tensor_scalar(
+                        out=y[:, j, :],
+                        in0=y[:, j, :],
+                        scalar1=rz[:, j : j + 1],
+                        scalar2=0.0,
+                        op0=ALU.mult,
+                        op1=ALU.add,
                     )
 
         def store(n, js):
@@ -318,6 +339,25 @@ def tile_attention_pa_t_w8_kernel(
         every = slice(0, TILES)
         last = NBLOCKS - 1
 
+        def normalize_late(n):
+            for j in range(TILES):
+                if NORM[n][j] == "gpsimd":
+                    normalize(n, slice(j, j + 1), "gpsimd")
+            store(n, every)
+
+        def normalize_soon(n):
+            for j in range(TILES):
+                if NORM[n][j] != "gpsimd":
+                    normalize(n, slice(j, j + 1), NORM[n][j])
+
+        def bias_rest(n):
+            add_bias(n, 0)
+            project(n, 2)
+            add_bias(n, 1)
+            project(n, 3)
+            add_bias(n, 2)
+            add_bias(n, 3)
+
         for half in range(2):
             widen(0, half)
             turn_query(0, half)
@@ -348,82 +388,94 @@ def tile_attention_pa_t_w8_kernel(
         quantize_context(1)
         for chunk in range(4):
             interleave(0, chunk, INTER[0][chunk])
+        widen(2, 0, 2)
         prepare_query_bits()
         prepare_context_bits(0)
 
-        for i in range(NBLOCKS):
-            if real(i + 1):
-                add_bias(i + 1, 0)
-                project(i + 1, 2)
-                add_bias(i + 1, 1)
+        for i in range(last - 1):
+            if real(i - 1):
+                exponent(i - 1, every)
+            if i > 0:
+                quantize_query(i + 2)
+                quantize_context(i + 2)
+                for t in range(2):
+                    project(i + 2, t)
+            if i % PER_BATCH == 0 and i > 0:
+                prepare_context_bits(i // PER_BATCH)
             quantize_q(i)
             for j in range(3):
                 score(i, j)
-            if real(i + 1):
-                project(i + 1, 3)
-                add_bias(i + 1, 2)
-                add_bias(i + 1, 3)
-                if i + 1 != last:
-                    for chunk in range(4):
-                        interleave(i + 1, chunk, INTER[i + 1][chunk])
-                if (i + 1) % PER_BATCH == 0:
-                    prepare_context_bits((i + 1) // PER_BATCH)
-            if i > 0 and real(i + 2):
-                if i == 1:
-                    quantize_context(2)
-                quantize_context(i + 2)
-            if i == last:
-                exponent(i - 1, every)
+            if i == 0:
+                bias_rest(1)
+            for chunk in range(4):
+                interleave(i + 1, chunk, INTER[i + 1][chunk])
+            if real(i - 2):
+                normalize_late(i - 2)
+            if real(i + 3) and i > 0:
+                scale_query(i + 3, 0)
             mask(i, 0)
             score(i, 3)
-            if i == 0:
-                widen(2, 0, 2)
-                for half in range(2):
-                    turn_query(2, half)
-                turn_context(2)
-                copy_context(2)
-            if i == last:
-                for j in range(TILES):
-                    js = slice(j, j + 1)
-                    row_min(i, js)
-                    if j == 2:
-                        invert(i - 1, every)
-                        for jj in range(TILES):
-                            normalize(i - 1, slice(jj, jj + 1), NORM[i - 1][jj])
-                        store(i - 1, every)
-                    exponent(i, js)
-                    if j + 1 < TILES:
-                        mask(i, j + 1)
-                for j in range(TILES):
-                    js = slice(j, j + 1)
-                    invert(i, js)
-                    normalize(i, js, NORM[i][j])
-                    store(i, js)
-                break
             for j in range(1, 4):
                 mask(i, j)
-            if real(i + 2):
-                scale_query(i + 2, 0)
-                scale_query(i + 2, 1)
+            if i == 0:
+                turn_query(2, 0)
+                turn_query(2, 1)
+                widen(3, 0, 2)
+                turn_context(2)
+                copy_context(2)
+                scale_query(2, 0)
+                scale_query(2, 1)
+                quantize_query(2)
+                quantize_context(2)
+                for t in range(2):
+                    project(2, t)
+                turn_query(3, 0)
+                turn_query(3, 1)
+                scale_query(3, 0)
+            bias_rest(i + 2)
             if real(i + 3):
+                scale_query(i + 3, 1)
                 turn_context(i + 3)
             if real(i - 1):
-                exponent(i - 1, every)
                 invert(i - 1, every)
-            if real(i + 2):
-                quantize_query(i + 2)
-                for t in range(2):
-                    project(i + 2, t)
             row_min(i, every)
-            if i + 1 == last:
-                for chunk in range(4):
-                    interleave(last, chunk, INTER[last][chunk])
+            if real(i + 4):
+                widen(i + 4, 0, 2)
             if real(i + 3):
-                widen(i + 3, 0, 2)
                 copy_context(i + 3)
+            if real(i + 4):
                 for half in range(2):
-                    turn_query(i + 3, half)
+                    turn_query(i + 4, half)
             if real(i - 1):
-                for j in range(TILES):
-                    normalize(i - 1, slice(j, j + 1), NORM[i - 1][j])
-                store(i - 1, every)
+                normalize_soon(i - 1)
+
+        a, z = last - 1, last
+        one = [slice(j, j + 1) for j in range(TILES)]
+        exponent(a - 1, every)
+        prepare_context_bits(a // PER_BATCH)
+        quantize_q(a)
+        for j in range(3):
+            score(a, j)
+        normalize_late(a - 2)
+        for chunk in range(4):
+            interleave(z, chunk, INTER[z][chunk])
+        quantize_q(z)
+        tail = [(n, j) for n in (a, z) for j in range(TILES)]
+        for step in range(len(tail) + 2):
+            if step < len(tail):
+                mask(*tail[step])
+            if step + 3 < len(tail):
+                score(*tail[step + 3])
+            if step == 1:
+                invert(a - 1, every)
+                normalize_soon(a - 1)
+                store(a - 1, every)
+            if 1 <= step <= len(tail):
+                n, j = tail[step - 1]
+                row_min(n, one[j])
+                exponent(n, one[j])
+            if step >= 2:
+                n, j = tail[step - 2]
+                invert(n, one[j])
+                normalize(n, one[j], NORM[n][j])
+                store(n, one[j])

from contextlib import ExitStack

import concourse.mybir as mybir
from concourse.masks import make_identity

F32 = mybir.dt.float32
BF16 = mybir.dt.bfloat16
I32 = mybir.dt.int32
U8 = mybir.dt.uint8
FP8 = mybir.dt.float8_e4m3fn
FP8X4 = mybir.dt.float8_e4m3fn_x4
ALU = mybir.AluOpType
ACT = mybir.ActivationFunctionType
AX = mybir.AxisListType

B, Q, K, D = 8, 1024, 512, 512
P = 128
NEG = 10000.0
FLOPS = 4 * B * Q * K * D
BYTES = B * Q * D + 2 * B * K * D + 4 * B * Q * K + D * D + D * D // 32

TILES = 4
NBLOCKS = B * Q // (P * TILES)
PER_BATCH = Q // (P * TILES)
INTER = (
    [["vector", "vector", "vector", "scalar"]]
    + [["gpsimd"] * 4] * (NBLOCKS - 3)
    + [["gpsimd", "gpsimd", "gpsimd", "scalar"]]
    + [["vector", "vector", "vector", "scalar"]]
)
NORM = (
    [["gpsimd", "scalar", "scalar", "scalar"]] * (NBLOCKS - 5)
    + [["scalar", "scalar", "scalar", "vector"]] * 2
    + [["scalar", "vector"] * 2]
    + [["scalar"] * 4]
    + [["scalar", "vector", "vector", "vector"]]
)


def tile_attention_pa_t_w8_kernel(
    tc, query_bytes, query_scale, context, query_bit, context_bit, W_in_words, W_in_scales, b_in, out
):
    nc = tc.nc
    with ExitStack() as ctx:
        const = ctx.enter_context(tc.tile_pool(name="const", bufs=1))
        loads = ctx.enter_context(tc.tile_pool(name="loads", bufs=B))
        work = ctx.enter_context(tc.tile_pool(name="work", bufs=2))
        psum = ctx.enter_context(tc.psum_pool(name="psum", bufs=2))
        ctx.enter_context(tc.manual_schedule())

        ident = const.tile([P, P], F32)
        make_identity(nc, ident[:])
        warm = const.tile([P, 1], F32)
        nc.vector.memset(warm[:], 0.0)
        nc.scalar.activation(out=warm[:], in_=warm[:], func=ACT.Exp)
        w_scales_raw = const.tile([P, D], U8, align_bytes=64)
        nc.vector.memset(w_scales_raw[:].bitcast(I32), 0)

        q_in = []
        c_in = []
        for b in range(B):
            bytes_tile = loads.tile([P, 2 * TILES, D], U8, align_bytes=64)
            rows_tile = loads.tile([P, K // P, D], BF16, align_bytes=64)
            q_in.append(bytes_tile)
            c_in.append(rows_tile)

        def load_query(b, lo, hi):
            src = query_bytes[b].rearrange("(p i) d -> p i d", i=2 * TILES)
            nc.sync.dma_start(out=q_in[b][:, lo:hi, :], in_=src[:, lo:hi, :])

        def load_context(b, lo, hi):
            src = context[b].rearrange("(a r) d -> r a d", r=P)
            nc.sync.dma_start(out=c_in[b][:, lo:hi, :], in_=src[:, lo:hi, :])

        k_scale = const.tile([P, 4], F32)
        w_raw = const.tile([P, D], I32, align_bytes=64)
        bias_bf = const.tile([P, 4], BF16)
        qbit_bf = const.tile([P, B, 2 * TILES], BF16)
        cbit = const.tile([P, B, K], BF16)

        def load_context_bits(b):
            nc.sync.dma_start(out=cbit[:, b, :], in_=context_bit[b].partition_broadcast(P))

        load_query(0, 0, 2)
        load_query(0, 2, TILES)
        nc.sync.dma_start(out=k_scale[:], in_=query_scale.rearrange("o a (p t) -> p (o a t)", t=4))
        load_query(0, TILES, 2 * TILES)
        nc.sync.dma_start(out=w_raw[:], in_=W_in_words[0].rearrange("p n t -> p (n t)").bitcast(I32))
        for quad in range(4):
            nc.sync.dma_start(
                out=w_scales_raw[32 * quad : 32 * quad + 4, :].bitcast(I32),
                in_=W_in_scales[0, 4 * quad : 4 * quad + 4, :].bitcast(I32),
            )
        load_context(0, 0, 4)
        load_query(1, 0, 2 * TILES)
        load_context(1, 0, 4)
        load_context_bits(1)
        nc.gpsimd.dma_start(out=bias_bf[:], in_=b_in.rearrange("(p t) -> p t", t=4))
        nc.gpsimd.dma_start(out=qbit_bf[:], in_=query_bit.rearrange("b (p i) -> p b i", i=2 * TILES))
        nc.gpsimd.dma_start(out=cbit[:, 0, :], in_=context_bit[0].partition_broadcast(P))
        for b in range(2, B):
            load_query(b, 0, 2 * TILES)
            load_context(b, 0, 4)
            load_context_bits(b)

        w_codes = const.tile([P, D], I32, align_bytes=64)
        w_scales = const.tile([P, D], U8, align_bytes=64)
        bias = const.tile([P, 4], F32)
        qbit = const.tile([P, B * 2 * TILES], F32)
        ncbit = const.tile([P, B, K], BF16)

        def prepare_weights():
            nc.vector.tensor_copy(
                out=w_codes[:].rearrange("p (t m) -> p t m", t=4), in_=w_raw[:].rearrange("p (m t) -> p t m", t=4)
            )
            nc.vector.tensor_copy(
                out=w_scales[:].rearrange("p (t m) -> p m t", t=4),
                in_=w_scales_raw[:].rearrange("p (m t) -> p m t", t=4),
            )
            nc.vector.tensor_copy(out=bias[:], in_=bias_bf[:])

        def prepare_query_bits():
            nc.vector.tensor_scalar(
                out=qbit[:],
                in0=qbit_bf[:].rearrange("p b i -> p (b i)"),
                scalar1=NEG,
                scalar2=None,
                op0=ALU.mult,
            )

        def prepare_context_bits(b):
            nc.vector.tensor_scalar(
                out=ncbit[:, b, :], in0=cbit[:, b, :], scalar1=-1.0, scalar2=1.0, op0=ALU.mult, op1=ALU.add
            )

        live = {}

        def widen(n, half, halves=1):
            b, h = divmod(n, PER_BATCH)
            if half == 0:
                xb = work.tile([P, TILES, D], BF16, align_bytes=64)
                live["xb", n] = xb
            js = slice(2 * half, 2 * (half + halves))
            src = slice(TILES * h + 2 * half, TILES * h + 2 * (half + halves))
            nc.scalar.copy(
                out=live["xb", n][:, js, :].rearrange("p i d -> p (i d)"),
                in_=q_in[b][:, src, :].rearrange("p i d -> p (i d)").bitcast(FP8),
            )

        def turn(rows, a0, tag):
            words = rows[:].bitcast(F32)
            xp = psum.tile([P, 2, 2, P], F32, tag=tag, bufs=1)
            for a in range(2):
                for u in range(2):
                    nc.tensor.transpose(xp[:, u, a, :], words[:, a0 + a, u : D // 2 : 2], ident[:])
            return xp

        def turn_query(n, half):
            live["xp", n, half] = turn(live["xb", n], 2 * half, "xp%d" % half)

        def scale_query(n, half):
            if half == 0:
                xt = work.tile([P, TILES * P, 4], BF16, align_bytes=64)
                live["xt", n] = xt
            xp = live.pop(("xp", n, half))
            nc.vector.tensor_tensor(
                out=live["xt", n][:, 256 * half : 256 * (half + 1), :].rearrange("p c (u e) -> p c u e", u=2),
                in0=xp[:].bitcast(BF16).rearrange("p u a (r e) -> p (a r) u e", e=2),
                in1=k_scale[:].rearrange("p (u e) -> p u e", u=2).unsqueeze(1).to_broadcast([P, 256, 2, 2]),
                op=ALU.mult,
            )

        def quantize_query(n):
            xt = live.pop(("xt", n))
            xc = work.tile([P, TILES * P], I32, align_bytes=64)
            xs = work.tile([P, TILES * P], U8, align_bytes=64)
            nc.vector.quantize_mx(out=xc[:].bitcast(FP8X4), scales=xs[:], in_=xt[:].rearrange("p c t -> p (c t)"))
            live["xq", n] = (xc, xs)

        def project(n, t):
            xc, xs = live["xq", n]
            qm = psum.tile([P, TILES * P], F32, bufs=2)
            nc.tensor.matmul_mx(
                out=qm[:],
                lhsT=w_codes[:, P * t : P * (t + 1)].bitcast(FP8X4),
                lhsT_scale=w_scales[:, P * t : P * (t + 1)],
                rhs=xc[:].bitcast(FP8X4),
                rhs_scale=xs[:],
                start=True,
                stop=True,
            )
            live["qm", n, t] = qm

        def add_bias(n, t):
            if t == 0:
                qp = work.tile([P, 4, TILES * P], BF16, align_bytes=64)
                live["qp", n] = qp
            qm = live.pop(("qm", n, t))
            nc.scalar.activation(
                out=live["qp", n][:, t, :], in_=qm[:], func=ACT.Identity, bias=bias[:, t : t + 1]
            )

        def interleave(n, chunk, engine):
            if chunk == 0:
                qi = work.tile([P, TILES * P, 4], BF16, align_bytes=64, bufs=1)
                live["qi", n] = qi
            cols = slice(P * chunk, P * (chunk + 1))
            dst = live["qi", n][:, cols, :]
            rows = live["qp", n][:, :, cols].rearrange("p t c -> p c t")
            if engine == "gpsimd":
                nc.gpsimd.tensor_scalar(
                    out=dst, in0=rows, scalar1=1.0, scalar2=0.0, op0=ALU.mult, op1=ALU.add
                )
            elif engine == "vector":
                nc.vector.tensor_copy(out=dst, in_=rows)
            else:
                nc.scalar.copy(out=dst, in_=rows)

        def quantize_q(n):
            qi = live.pop(("qi", n))
            qc = work.tile([P, TILES * P], I32, align_bytes=64)
            qs = work.tile([P, TILES * P], U8, align_bytes=64)
            nc.vector.quantize_mx(
                out=qc[:].bitcast(FP8X4), scales=qs[:], in_=qi[:].rearrange("p c t -> p (c t)")
            )
            live["qq", n] = (qc, qs)

        def score(n, j):
            qc, qs = live["qq", n]
            cc, cs = live["cq", n // PER_BATCH]
            sm = psum.tile([P, K], F32, bufs=3)
            nc.tensor.matmul_mx(
                out=sm[:],
                lhsT=qc[:, P * j : P * (j + 1)].bitcast(FP8X4),
                lhsT_scale=qs[:, P * j : P * (j + 1)],
                rhs=cc[:].bitcast(FP8X4),
                rhs_scale=cs[:],
                start=True,
                stop=True,
            )
            live["sm", n, j] = sm

        def mask(n, j):
            b, h = divmod(n, PER_BATCH)
            if j == 0:
                y = work.tile([P, TILES, K], F32, bufs=5)
                live["y", n] = y
            sm = live.pop(("sm", n, j))
            column = b * 2 * TILES + TILES * h + j
            nc.vector.scalar_tensor_tensor(
                out=live["y", n][:, j, :],
                in0=ncbit[:, b, :],
                scalar=qbit[:, column : column + 1],
                in1=sm[:],
                op0=ALU.mult,
                op1=ALU.subtract,
            )

        def row_min(n, js):
            if js.start == 0:
                ymin = work.tile([P, TILES], F32, bufs=3)
                live["ymin", n] = ymin
            nc.vector.tensor_reduce(out=live["ymin", n][:, js], in_=live["y", n][:, js, :], axis=AX.X, op=ALU.min)

        def exponent(n, js):
            y = live["y", n]
            if js.start == 0:
                z = work.tile([P, TILES], F32, bufs=3)
                live["z", n] = z
            for j in range(js.start, js.stop):
                nc.scalar.activation(
                    out=y[:, j, :],
                    in_=y[:, j, :],
                    func=ACT.Exp,
                    bias=live["ymin", n][:, j : j + 1],
                    scale=-1.0,
                    accum_out=live["z", n][:, j : j + 1],
                )

        def invert(n, js):
            if js.start == 0:
                rz = work.tile([P, TILES], F32, bufs=4)
                live["rz", n] = rz
            nc.vector.reciprocal(out=live["rz", n][:, js], in_=live["z", n][:, js])

        def normalize(n, js, engine):
            y = live["y", n]
            rz = live["rz", n]
            for j in range(js.start, js.stop):
                if engine == "scalar":
                    nc.scalar.activation(out=y[:, j, :], in_=y[:, j, :], func=ACT.Copy, scale=rz[:, j : j + 1])
                elif engine == "vector":
                    nc.vector.tensor_scalar(
                        out=y[:, j, :], in0=y[:, j, :], scalar1=rz[:, j : j + 1], scalar2=None, op0=ALU.mult
                    )
                else:
                    nc.gpsimd.tensor_scalar(
                        out=y[:, j, :],
                        in0=y[:, j, :],
                        scalar1=rz[:, j : j + 1],
                        scalar2=0.0,
                        op0=ALU.mult,
                        op1=ALU.add,
                    )

        def store(n, js):
            b, h = divmod(n, PER_BATCH)
            dst = out[b].rearrange("(p i) j -> p i j", i=2 * TILES)
            nc.sync.dma_start(
                out=dst[:, TILES * h + js.start : TILES * h + js.stop, :], in_=live["y", n][:, js, :]
            )

        def turn_context(m):
            b, h = divmod(m, 2)
            live["cp", m] = turn(c_in[b], 2 * h, "cp")

        def copy_context(m):
            ct = work.tile([P, 2 * P * 4], BF16, align_bytes=64)
            nc.scalar.copy(
                out=ct[:].bitcast(F32).rearrange("p (c u) -> p c u", u=2),
                in_=live.pop(("cp", m))[:].rearrange("p u a r -> p (a r) u"),
            )
            live["ct", m] = ct

        def quantize_context(m):
            b, h = divmod(m, 2)
            if h == 0:
                cc = work.tile([P, K], I32, align_bytes=64, bufs=3)
                cs = work.tile([P, K], U8, align_bytes=64, bufs=3)
                live["cq", b] = (cc, cs)
            cc, cs = live["cq", b]
            ct = live.pop(("ct", m))
            cols = slice(2 * P * h, 2 * P * (h + 1))
            nc.vector.quantize_mx(out=cc[:, cols].bitcast(FP8X4), scales=cs[:, cols], in_=ct[:])

        def real(n):
            return 0 <= n < NBLOCKS

        every = slice(0, TILES)
        last = NBLOCKS - 1

        def normalize_late(n):
            for j in range(TILES):
                if NORM[n][j] == "gpsimd":
                    normalize(n, slice(j, j + 1), "gpsimd")
            store(n, every)

        def normalize_soon(n):
            for j in range(TILES):
                if NORM[n][j] != "gpsimd":
                    normalize(n, slice(j, j + 1), NORM[n][j])

        def bias_rest(n):
            add_bias(n, 0)
            project(n, 2)
            add_bias(n, 1)
            project(n, 3)
            add_bias(n, 2)
            add_bias(n, 3)

        for half in range(2):
            widen(0, half)
            turn_query(0, half)
            scale_query(0, half)
        widen(1, 0, 2)
        turn_context(0)
        copy_context(0)
        prepare_weights()
        quantize_query(0)
        turn_query(1, 0)
        scale_query(1, 0)
        for t in range(2):
            project(0, t)
        turn_query(1, 1)
        scale_query(1, 1)
        turn_context(1)
        add_bias(0, 0)
        project(0, 2)
        add_bias(0, 1)
        project(0, 3)
        copy_context(1)
        quantize_context(0)
        quantize_query(1)
        add_bias(0, 2)
        add_bias(0, 3)
        for t in range(2):
            project(1, t)
        quantize_context(1)
        for chunk in range(4):
            interleave(0, chunk, INTER[0][chunk])
        widen(2, 0, 2)
        prepare_query_bits()
        prepare_context_bits(0)

        for i in range(last - 1):
            if real(i - 1):
                exponent(i - 1, every)
            if i > 0:
                quantize_query(i + 2)
                quantize_context(i + 2)
                for t in range(2):
                    project(i + 2, t)
            if i % PER_BATCH == 0 and i > 0:
                prepare_context_bits(i // PER_BATCH)
            quantize_q(i)
            for j in range(3):
                score(i, j)
            if i == 0:
                bias_rest(1)
            for chunk in range(4):
                interleave(i + 1, chunk, INTER[i + 1][chunk])
            if real(i - 2):
                normalize_late(i - 2)
            if real(i + 3) and i > 0:
                scale_query(i + 3, 0)
            mask(i, 0)
            score(i, 3)
            for j in range(1, 4):
                mask(i, j)
            if i == 0:
                turn_query(2, 0)
                turn_query(2, 1)
                widen(3, 0, 2)
                turn_context(2)
                copy_context(2)
                scale_query(2, 0)
                scale_query(2, 1)
                quantize_query(2)
                quantize_context(2)
                for t in range(2):
                    project(2, t)
                turn_query(3, 0)
                turn_query(3, 1)
                scale_query(3, 0)
            bias_rest(i + 2)
            if real(i + 3):
                scale_query(i + 3, 1)
                turn_context(i + 3)
            if real(i - 1):
                invert(i - 1, every)
            row_min(i, every)
            if real(i + 4):
                widen(i + 4, 0, 2)
            if real(i + 3):
                copy_context(i + 3)
            if real(i + 4):
                for half in range(2):
                    turn_query(i + 4, half)
            if real(i - 1):
                normalize_soon(i - 1)

        a, z = last - 1, last
        one = [slice(j, j + 1) for j in range(TILES)]
        exponent(a - 1, every)
        prepare_context_bits(a // PER_BATCH)
        quantize_q(a)
        for j in range(3):
            score(a, j)
        normalize_late(a - 2)
        for chunk in range(4):
            interleave(z, chunk, INTER[z][chunk])
        quantize_q(z)
        tail = [(n, j) for n in (a, z) for j in range(TILES)]
        for step in range(len(tail) + 2):
            if step < len(tail):
                mask(*tail[step])
            if step + 3 < len(tail):
                score(*tail[step + 3])
            if step == 1:
                invert(a - 1, every)
                normalize_soon(a - 1)
                store(a - 1, every)
            if 1 <= step <= len(tail):
                n, j = tail[step - 1]
                row_min(n, one[j])
                exponent(n, one[j])
            if step >= 2:
                n, j = tail[step - 2]
                invert(n, one[j])
                normalize(n, one[j], NORM[n][j])
                store(n, one[j])
